import numpy as np
import ml_dtypes

BF16 = ml_dtypes.bfloat16


def bf(x):
    return np.asarray(x, np.float32).astype(BF16)


def f32(x):
    return np.asarray(x, np.float32)


def f64(x):
    return np.asarray(x).astype(np.float64)


def striped(idx):
    return np.tile(idx.reshape(-1, 16).T, (8, 1))


C, S, KN, DK, H, RUNS, N = 256, 512, 9, 32, 256, 18, 4608


def setup_inputs():
    return {
        "h": f32(np.random.standard_normal((C, S))),
        "wq": bf(np.random.standard_normal((C, C)) / np.sqrt(C)),
        "bq": f32(0.1 * np.random.standard_normal((C, 1))),
        "wk": bf(np.random.standard_normal((C, C)) / np.sqrt(C)),
        "bk": f32(0.1 * np.random.standard_normal((C, 1))),
        "offs": striped(np.concatenate([np.random.permutation(S)[:H] for _ in range(RUNS)])),
    }


def reference(h, wq, bq, wk, bk, offs):
    idx = offs[:16].T.reshape(-1)
    q = (f64(wq).T @ f64(h) + f64(bq)) / np.sqrt(DK)
    key = f64(wk).T @ f64(h) + f64(bk)
    return key[:, idx] * np.tile(q, (1, KN))

@@ -1,0 +1,82 @@
+import math
+
+import concourse.mybir as mybir
+
+P = 128
+C = 256
+S = 512
+NEIGHBOURS = 9
+HEAD = 32
+N = NEIGHBOURS * S
+BLOCKS = C // P
+LIST_COLS = S // 16
+
+FLOPS = 2 * 2 * C * C * S + C * N
+
+F32 = mybir.dt.float32
+BF16 = mybir.dt.bfloat16
+U16 = mybir.dt.uint16
+IDENTITY = mybir.ActivationFunctionType.Identity
+MULT = mybir.AluOpType.mult
+
+
+def tile_attentionfusion_kernel(tc, h, wq, bq, wk, bk, offs, out):
+    nc = tc.nc
+    scale = 1.0 / math.sqrt(HEAD)
+
+    with (
+        tc.tile_pool(name="held", bufs=1) as held,
+        tc.tile_pool(name="products", bufs=4) as products,
+        tc.psum_pool(name="banks", bufs=4) as banks,
+    ):
+        h_f32 = [held.tile([P, S], F32, name=f"h_f32_{i}") for i in range(BLOCKS)]
+        nc.sync.dma_start(h_f32[0][:], h[0:P, :])
+        nc.scalar.dma_start(h_f32[1][:], h[P : 2 * P, :])
+        wk_sb = held.tile([P, BLOCKS, C], BF16, name="wk_sb")
+        wq_sb = held.tile([P, BLOCKS, C], BF16, name="wq_sb")
+        nc.sync.dma_start(wk_sb[:], wk.rearrange("(i p) c -> p i c", p=P))
+        nc.scalar.dma_start(wq_sb[:], wq.rearrange("(i p) c -> p i c", p=P))
+        offsets = held.tile([P, N // 16], U16, name="offsets")
+        nc.sync.dma_start(offsets[:], offs)
+        bk_sb = [held.tile([P, 1], F32, name=f"bk_sb_{b}") for b in range(BLOCKS)]
+        bq_sb = [held.tile([P, 1], F32, name=f"bq_sb_{b}") for b in range(BLOCKS)]
+        for b in range(BLOCKS):
+            nc.gpsimd.dma_start(bk_sb[b][:], bk[b * P : (b + 1) * P, :])
+            nc.gpsimd.dma_start(bq_sb[b][:], bq[b * P : (b + 1) * P, :])
+
+        bq_scaled = [held.tile([P, 1], F32, name=f"bq_scaled_{b}") for b in range(BLOCKS)]
+        for b in range(BLOCKS):
+            nc.gpsimd.tensor_scalar_mul(bq_scaled[b][:], bq_sb[b][:], scale)
+
+        h_bf = [held.tile([P, S], BF16, name=f"h_bf_{i}") for i in range(BLOCKS)]
+        for i in range(BLOCKS):
+            nc.vector.tensor_copy(h_bf[i][:], h_f32[i][:])
+
+        for b in range(BLOCKS):
+            channels = slice(b * P, (b + 1) * P)
+
+            key_ps = banks.tile([P, S], F32, name="key_ps")
+            q_ps = banks.tile([P, S], F32, name="q_ps")
+            for i in range(BLOCKS):
+                nc.tensor.matmul(
+                    key_ps[:], wk_sb[:, i, channels], h_bf[i][:], start=(i == 0), stop=(i == BLOCKS - 1)
+                )
+            for i in range(BLOCKS):
+                nc.tensor.matmul(
+                    q_ps[:], wq_sb[:, i, channels], h_bf[i][:], start=(i == 0), stop=(i == BLOCKS - 1)
+                )
+            key = held.tile([P, S], F32, name=f"key_{b}")
+            q = held.tile([P, S], F32, name=f"q_{b}")
+            nc.scalar.activation(key[:], key_ps[:], IDENTITY, bias=bk_sb[b][:])
+            nc.scalar.activation(q[:], q_ps[:], IDENTITY, bias=bq_scaled[b][:], scale=scale)
+
+            for t in range(NEIGHBOURS):
+                product = products.tile([P, S], F32, name="product")
+                nc.vector.tensor_tensor(
+                    product[:],
+                    key[:].indirect(offsets[:, t * LIST_COLS : (t + 1) * LIST_COLS]),
+                    q[:],
+                    MULT,
+                )
+                queue = nc.sync if t % 2 == 0 else nc.scalar
+                queue.dma_start(out[channels, t * S : (t + 1) * S], product[:])

@@ -27,7 +27,7 @@ def tile_attentionfusion_kernel(tc, h, wq, bq, wk, bk, offs, out):
     with (
         tc.tile_pool(name="held", bufs=1) as held,
         tc.tile_pool(name="products", bufs=4) as products,
-        tc.psum_pool(name="banks", bufs=4) as banks,
+        tc.psum_pool(name="banks", bufs=2) as banks,
     ):
         h_f32 = [held.tile([P, S], F32, name=f"h_f32_{i}") for i in range(BLOCKS)]
         nc.sync.dma_start(h_f32[0][:], h[0:P, :])
@@ -36,13 +36,13 @@ def tile_attentionfusion_kernel(tc, h, wq, bq, wk, bk, offs, out):
         wq_sb = held.tile([P, BLOCKS, C], BF16, name="wq_sb")
         nc.sync.dma_start(wk_sb[:], wk.rearrange("(i p) c -> p i c", p=P))
         nc.scalar.dma_start(wq_sb[:], wq.rearrange("(i p) c -> p i c", p=P))
-        offsets = held.tile([P, N // 16], U16, name="offsets")
-        nc.sync.dma_start(offsets[:], offs)
         bk_sb = [held.tile([P, 1], F32, name=f"bk_sb_{b}") for b in range(BLOCKS)]
         bq_sb = [held.tile([P, 1], F32, name=f"bq_sb_{b}") for b in range(BLOCKS)]
         for b in range(BLOCKS):
-            nc.gpsimd.dma_start(bk_sb[b][:], bk[b * P : (b + 1) * P, :])
-            nc.gpsimd.dma_start(bq_sb[b][:], bq[b * P : (b + 1) * P, :])
+            nc.sync.dma_start(bk_sb[b][:], bk[b * P : (b + 1) * P, :])
+            nc.scalar.dma_start(bq_sb[b][:], bq[b * P : (b + 1) * P, :])
+        offsets = held.tile([P, N // 16], U16, name="offsets")
+        nc.sync.dma_start(offsets[:], offs)
 
         bq_scaled = [held.tile([P, 1], F32, name=f"bq_scaled_{b}") for b in range(BLOCKS)]
         for b in range(BLOCKS):

@@ -27,7 +27,7 @@ def tile_attentionfusion_kernel(tc, h, wq, bq, wk, bk, offs, out):
     with (
         tc.tile_pool(name="held", bufs=1) as held,
         tc.tile_pool(name="products", bufs=4) as products,
-        tc.psum_pool(name="banks", bufs=2) as banks,
+        tc.psum_pool(name="banks", bufs=1) as banks,
     ):
         h_f32 = [held.tile([P, S], F32, name=f"h_f32_{i}") for i in range(BLOCKS)]
         nc.sync.dma_start(h_f32[0][:], h[0:P, :])

@@ -11,6 +11,8 @@ N = NEIGHBOURS * S
 BLOCKS = C // P
 LIST_COLS = S // 16
 
+WARM_UP = 4
+
 FLOPS = 2 * 2 * C * C * S + C * N
 
 F32 = mybir.dt.float32
@@ -18,6 +20,7 @@ BF16 = mybir.dt.bfloat16
 U16 = mybir.dt.uint16
 IDENTITY = mybir.ActivationFunctionType.Identity
 MULT = mybir.AluOpType.mult
+ADD = mybir.AluOpType.add
 
 
 def tile_attentionfusion_kernel(tc, h, wq, bq, wk, bk, offs, out):
@@ -27,22 +30,29 @@ def tile_attentionfusion_kernel(tc, h, wq, bq, wk, bk, offs, out):
     with (
         tc.tile_pool(name="held", bufs=1) as held,
         tc.tile_pool(name="products", bufs=4) as products,
-        tc.psum_pool(name="banks", bufs=1) as banks,
+        tc.psum_pool(name="banks", bufs=2) as banks,
     ):
         h_f32 = [held.tile([P, S], F32, name=f"h_f32_{i}") for i in range(BLOCKS)]
-        nc.sync.dma_start(h_f32[0][:], h[0:P, :])
-        nc.scalar.dma_start(h_f32[1][:], h[P : 2 * P, :])
+        h_view = h.rearrange("(p i) s -> p i s", i=BLOCKS)
+        nc.sync.dma_start(h_f32[0][:], h_view[:, 0, :])
+        nc.scalar.dma_start(h_f32[1][:], h_view[:, 1, :])
         wk_sb = held.tile([P, BLOCKS, C], BF16, name="wk_sb")
         wq_sb = held.tile([P, BLOCKS, C], BF16, name="wq_sb")
-        nc.sync.dma_start(wk_sb[:], wk.rearrange("(i p) c -> p i c", p=P))
-        nc.scalar.dma_start(wq_sb[:], wq.rearrange("(i p) c -> p i c", p=P))
+        nc.sync.dma_start(wk_sb[:], wk.rearrange("(p i) c -> p i c", i=BLOCKS))
+        nc.scalar.dma_start(wq_sb[:], wq.rearrange("(p i) c -> p i c", i=BLOCKS))
+        offsets = held.tile([P, N // 16], U16, name="offsets")
+        nc.sync.dma_start(offsets[:], offs)
         bk_sb = [held.tile([P, 1], F32, name=f"bk_sb_{b}") for b in range(BLOCKS)]
         bq_sb = [held.tile([P, 1], F32, name=f"bq_sb_{b}") for b in range(BLOCKS)]
         for b in range(BLOCKS):
             nc.sync.dma_start(bk_sb[b][:], bk[b * P : (b + 1) * P, :])
             nc.scalar.dma_start(bq_sb[b][:], bq[b * P : (b + 1) * P, :])
-        offsets = held.tile([P, N // 16], U16, name="offsets")
-        nc.sync.dma_start(offsets[:], offs)
+
+        zeros = held.tile([P, S], BF16, name="zeros")
+        nc.vector.memset(zeros[:], 0.0)
+        warm_ps = banks.tile([P, S], F32, name="warm_ps")
+        for repeat in range(WARM_UP):
+            nc.tensor.matmul(warm_ps[:], zeros[:, 0:P], zeros[:], start=True, stop=True)
 
         bq_scaled = [held.tile([P, 1], F32, name=f"bq_scaled_{b}") for b in range(BLOCKS)]
         for b in range(BLOCKS):
@@ -67,8 +77,12 @@ def tile_attentionfusion_kernel(tc, h, wq, bq, wk, bk, offs, out):
                 )
             key = held.tile([P, S], F32, name=f"key_{b}")
             q = held.tile([P, S], F32, name=f"q_{b}")
-            nc.scalar.activation(key[:], key_ps[:], IDENTITY, bias=bk_sb[b][:])
-            nc.scalar.activation(q[:], q_ps[:], IDENTITY, bias=bq_scaled[b][:], scale=scale)
+            if b == 0:
+                nc.vector.tensor_scalar_add(key[:], key_ps[:], bk_sb[b][:])
+                nc.vector.tensor_scalar(q[:], q_ps[:], bq_sb[b][:], scale, ADD, MULT)
+            else:
+                nc.scalar.activation(key[:], key_ps[:], IDENTITY, bias=bk_sb[b][:])
+                nc.scalar.activation(q[:], q_ps[:], IDENTITY, bias=bq_scaled[b][:], scale=scale)
 
             for t in range(NEIGHBOURS):
                 product = products.tile([P, S], F32, name="product")
@@ -78,5 +92,4 @@ def tile_attentionfusion_kernel(tc, h, wq, bq, wk, bk, offs, out):
                     q[:],
                     MULT,
                 )
-                queue = nc.sync if t % 2 == 0 else nc.scalar
-                queue.dma_start(out[channels, t * S : (t + 1) * S], product[:])
+                nc.sync.dma_start(out[channels, t * S : (t + 1) * S], product[:])

@@ -42,11 +42,10 @@ def tile_attentionfusion_kernel(tc, h, wq, bq, wk, bk, offs, out):
         nc.scalar.dma_start(wq_sb[:], wq.rearrange("(p i) c -> p i c", i=BLOCKS))
         offsets = held.tile([P, N // 16], U16, name="offsets")
         nc.sync.dma_start(offsets[:], offs)
-        bk_sb = [held.tile([P, 1], F32, name=f"bk_sb_{b}") for b in range(BLOCKS)]
-        bq_sb = [held.tile([P, 1], F32, name=f"bq_sb_{b}") for b in range(BLOCKS)]
-        for b in range(BLOCKS):
-            nc.sync.dma_start(bk_sb[b][:], bk[b * P : (b + 1) * P, :])
-            nc.scalar.dma_start(bq_sb[b][:], bq[b * P : (b + 1) * P, :])
+        bk_sb = held.tile([P, BLOCKS], F32, name="bk_sb")
+        bq_sb = held.tile([P, BLOCKS], F32, name="bq_sb")
+        nc.scalar.dma_start(bk_sb[:], bk.rearrange("(b p) o -> p (b o)", p=P))
+        nc.gpsimd.dma_start(bq_sb[:], bq.rearrange("(b p) o -> p (b o)", p=P))
 
         zeros = held.tile([P, S], BF16, name="zeros")
         nc.vector.memset(zeros[:], 0.0)
@@ -54,9 +53,8 @@ def tile_attentionfusion_kernel(tc, h, wq, bq, wk, bk, offs, out):
         for repeat in range(WARM_UP):
             nc.tensor.matmul(warm_ps[:], zeros[:, 0:P], zeros[:], start=True, stop=True)
 
-        bq_scaled = [held.tile([P, 1], F32, name=f"bq_scaled_{b}") for b in range(BLOCKS)]
-        for b in range(BLOCKS):
-            nc.gpsimd.tensor_scalar_mul(bq_scaled[b][:], bq_sb[b][:], scale)
+        bq_scaled = held.tile([P, BLOCKS], F32, name="bq_scaled")
+        nc.gpsimd.tensor_scalar_mul(bq_scaled[:], bq_sb[:], scale)
 
         h_bf = [held.tile([P, S], BF16, name=f"h_bf_{i}") for i in range(BLOCKS)]
         for i in range(BLOCKS):
@@ -78,11 +76,11 @@ def tile_attentionfusion_kernel(tc, h, wq, bq, wk, bk, offs, out):
             key = held.tile([P, S], F32, name=f"key_{b}")
             q = held.tile([P, S], F32, name=f"q_{b}")
             if b == 0:
-                nc.vector.tensor_scalar_add(key[:], key_ps[:], bk_sb[b][:])
-                nc.vector.tensor_scalar(q[:], q_ps[:], bq_sb[b][:], scale, ADD, MULT)
+                nc.vector.tensor_scalar_add(key[:], key_ps[:], bk_sb[:, b : b + 1])
+                nc.vector.tensor_scalar(q[:], q_ps[:], bq_sb[:, b : b + 1], scale, ADD, MULT)
             else:
-                nc.scalar.activation(key[:], key_ps[:], IDENTITY, bias=bk_sb[b][:])
-                nc.scalar.activation(q[:], q_ps[:], IDENTITY, bias=bq_scaled[b][:], scale=scale)
+                nc.scalar.activation(key[:], key_ps[:], IDENTITY, bias=bk_sb[:, b : b + 1])
+                nc.scalar.activation(q[:], q_ps[:], IDENTITY, bias=bq_scaled[:, b : b + 1], scale=scale)
 
             for t in range(NEIGHBOURS):
                 product = products.tile([P, S], F32, name="product")

@@ -10,6 +10,8 @@ HEAD = 32
 N = NEIGHBOURS * S
 BLOCKS = C // P
 LIST_COLS = S // 16
+PAIR = 2
+STORES = BLOCKS * ((NEIGHBOURS + PAIR - 1) // PAIR)
 
 WARM_UP = 4
 
@@ -29,7 +31,7 @@ def tile_attentionfusion_kernel(tc, h, wq, bq, wk, bk, offs, out):
 
     with (
         tc.tile_pool(name="held", bufs=1) as held,
-        tc.tile_pool(name="products", bufs=4) as products,
+        tc.tile_pool(name="products", bufs=STORES) as products,
         tc.psum_pool(name="banks", bufs=2) as banks,
     ):
         h_f32 = [held.tile([P, S], F32, name=f"h_f32_{i}") for i in range(BLOCKS)]
@@ -82,12 +84,15 @@ def tile_attentionfusion_kernel(tc, h, wq, bq, wk, bk, offs, out):
                 nc.scalar.activation(key[:], key_ps[:], IDENTITY, bias=bk_sb[:, b : b + 1])
                 nc.scalar.activation(q[:], q_ps[:], IDENTITY, bias=bq_scaled[:, b : b + 1], scale=scale)
 
-            for t in range(NEIGHBOURS):
-                product = products.tile([P, S], F32, name="product")
-                nc.vector.tensor_tensor(
-                    product[:],
-                    key[:].indirect(offsets[:, t * LIST_COLS : (t + 1) * LIST_COLS]),
-                    q[:],
-                    MULT,
-                )
-                nc.sync.dma_start(out[channels, t * S : (t + 1) * S], product[:])
+            for first in range(0, NEIGHBOURS, PAIR):
+                together = min(PAIR, NEIGHBOURS - first)
+                product = products.tile([P, together * S], F32, name="product")
+                for u in range(together):
+                    t = first + u
+                    nc.vector.tensor_tensor(
+                        product[:, u * S : (u + 1) * S],
+                        key[:].indirect(offsets[:, t * LIST_COLS : (t + 1) * LIST_COLS]),
+                        q[:],
+                        MULT,
+                    )
+                nc.sync.dma_start(out[channels, first * S : (first + together) * S], product[:])

@@ -11,6 +11,7 @@ N = NEIGHBOURS * S
 BLOCKS = C // P
 LIST_COLS = S // 16
 PAIR = 2
+HALF = S // 2
 STORES = BLOCKS * ((NEIGHBOURS + PAIR - 1) // PAIR)
 
 WARM_UP = 4
@@ -32,12 +33,12 @@ def tile_attentionfusion_kernel(tc, h, wq, bq, wk, bk, offs, out):
     with (
         tc.tile_pool(name="held", bufs=1) as held,
         tc.tile_pool(name="products", bufs=STORES) as products,
-        tc.psum_pool(name="banks", bufs=2) as banks,
+        tc.psum_pool(name="banks", bufs=1) as banks,
     ):
-        h_f32 = [held.tile([P, S], F32, name=f"h_f32_{i}") for i in range(BLOCKS)]
+        h_f32 = held.tile([P, BLOCKS, S], F32, name="h_f32")
         h_view = h.rearrange("(p i) s -> p i s", i=BLOCKS)
-        nc.sync.dma_start(h_f32[0][:], h_view[:, 0, :])
-        nc.scalar.dma_start(h_f32[1][:], h_view[:, 1, :])
+        nc.sync.dma_start(h_f32[:, 0, :], h_view[:, 0, :])
+        nc.scalar.dma_start(h_f32[:, 1, :], h_view[:, 1, :])
         wk_sb = held.tile([P, BLOCKS, C], BF16, name="wk_sb")
         wq_sb = held.tile([P, BLOCKS, C], BF16, name="wq_sb")
         nc.sync.dma_start(wk_sb[:], wk.rearrange("(p i) c -> p i c", i=BLOCKS))
@@ -58,31 +59,31 @@ def tile_attentionfusion_kernel(tc, h, wq, bq, wk, bk, offs, out):
         bq_scaled = held.tile([P, BLOCKS], F32, name="bq_scaled")
         nc.gpsimd.tensor_scalar_mul(bq_scaled[:], bq_sb[:], scale)
 
-        h_bf = [held.tile([P, S], BF16, name=f"h_bf_{i}") for i in range(BLOCKS)]
-        for i in range(BLOCKS):
-            nc.vector.tensor_copy(h_bf[i][:], h_f32[i][:])
+        halves = [slice(0, HALF), slice(HALF, S)]
+        h_bf = held.tile([P, BLOCKS, S], BF16, name="h_bf")
+        for pixels in halves:
+            nc.vector.tensor_copy(h_bf[:, :, pixels], h_f32[:, :, pixels])
 
         for b in range(BLOCKS):
             channels = slice(b * P, (b + 1) * P)
 
-            key_ps = banks.tile([P, S], F32, name="key_ps")
-            q_ps = banks.tile([P, S], F32, name="q_ps")
-            for i in range(BLOCKS):
-                nc.tensor.matmul(
-                    key_ps[:], wk_sb[:, i, channels], h_bf[i][:], start=(i == 0), stop=(i == BLOCKS - 1)
-                )
-            for i in range(BLOCKS):
-                nc.tensor.matmul(
-                    q_ps[:], wq_sb[:, i, channels], h_bf[i][:], start=(i == 0), stop=(i == BLOCKS - 1)
-                )
             key = held.tile([P, S], F32, name=f"key_{b}")
             q = held.tile([P, S], F32, name=f"q_{b}")
-            if b == 0:
-                nc.vector.tensor_scalar_add(key[:], key_ps[:], bk_sb[:, b : b + 1])
-                nc.vector.tensor_scalar(q[:], q_ps[:], bq_sb[:, b : b + 1], scale, ADD, MULT)
-            else:
-                nc.scalar.activation(key[:], key_ps[:], IDENTITY, bias=bk_sb[:, b : b + 1])
-                nc.scalar.activation(q[:], q_ps[:], IDENTITY, bias=bq_scaled[:, b : b + 1], scale=scale)
+            for n, pixels in enumerate(halves if b == 0 else [slice(0, S)]):
+                width = pixels.stop - pixels.start
+                key_ps = banks.tile([P, width], F32, name=f"key_ps_{b}_{n}")
+                q_ps = banks.tile([P, width], F32, name=f"q_ps_{b}_{n}")
+                for bank, weights in ((key_ps, wk_sb), (q_ps, wq_sb)):
+                    for i in range(BLOCKS):
+                        nc.tensor.matmul(
+                            bank[:], weights[:, i, channels], h_bf[:, i, pixels], start=(i == 0), stop=(i == BLOCKS - 1)
+                        )
+                if b == 0:
+                    nc.vector.tensor_scalar_add(key[:, pixels], key_ps[:], bk_sb[:, b : b + 1])
+                    nc.vector.tensor_scalar(q[:, pixels], q_ps[:], bq_sb[:, b : b + 1], scale, ADD, MULT)
+                else:
+                    nc.scalar.activation(key[:, pixels], key_ps[:], IDENTITY, bias=bk_sb[:, b : b + 1])
+                    nc.scalar.activation(q[:, pixels], q_ps[:], IDENTITY, bias=bq_scaled[:, b : b + 1], scale=scale)
 
             for first in range(0, NEIGHBOURS, PAIR):
                 together = min(PAIR, NEIGHBOURS - first)

@@ -36,19 +36,17 @@ def tile_attentionfusion_kernel(tc, h, wq, bq, wk, bk, offs, out):
         tc.psum_pool(name="banks", bufs=1) as banks,
     ):
         h_f32 = held.tile([P, BLOCKS, S], F32, name="h_f32")
-        h_view = h.rearrange("(p i) s -> p i s", i=BLOCKS)
-        nc.sync.dma_start(h_f32[:, 0, :], h_view[:, 0, :])
-        nc.scalar.dma_start(h_f32[:, 1, :], h_view[:, 1, :])
+        nc.sync.dma_start(h_f32[:], h.rearrange("(p i) s -> p i s", i=BLOCKS))
         wk_sb = held.tile([P, BLOCKS, C], BF16, name="wk_sb")
         wq_sb = held.tile([P, BLOCKS, C], BF16, name="wq_sb")
-        nc.sync.dma_start(wk_sb[:], wk.rearrange("(p i) c -> p i c", i=BLOCKS))
+        nc.scalar.dma_start(wk_sb[:], wk.rearrange("(p i) c -> p i c", i=BLOCKS))
         nc.scalar.dma_start(wq_sb[:], wq.rearrange("(p i) c -> p i c", i=BLOCKS))
-        offsets = held.tile([P, N // 16], U16, name="offsets")
-        nc.sync.dma_start(offsets[:], offs)
         bk_sb = held.tile([P, BLOCKS], F32, name="bk_sb")
         bq_sb = held.tile([P, BLOCKS], F32, name="bq_sb")
         nc.scalar.dma_start(bk_sb[:], bk.rearrange("(b p) o -> p (b o)", p=P))
         nc.gpsimd.dma_start(bq_sb[:], bq.rearrange("(b p) o -> p (b o)", p=P))
+        offsets = held.tile([P, N // 16], U16, name="offsets")
+        nc.sync.dma_start(offsets[:], offs)
 
         zeros = held.tile([P, S], BF16, name="zeros")
         nc.vector.memset(zeros[:], 0.0)

@@ -14,6 +14,7 @@ PAIR = 2
 HALF = S // 2
 STORES = BLOCKS * ((NEIGHBOURS + PAIR - 1) // PAIR)
 
+SQUARE = 32
 WARM_UP = 4
 
 FLOPS = 2 * 2 * C * C * S + C * N
@@ -35,16 +36,18 @@ def tile_attentionfusion_kernel(tc, h, wq, bq, wk, bk, offs, out):
         tc.tile_pool(name="products", bufs=STORES) as products,
         tc.psum_pool(name="banks", bufs=1) as banks,
     ):
+        bias_rows = held.tile([P, 2, BLOCKS, SQUARE], F32, name="bias_rows", align_bytes=64)
+        nc.vector.memset(bias_rows[:], 0.0)
+        first_rows = bias_rows[:].rearrange("(g r) m b x -> g r m b x", r=SQUARE)[:, 0]
+
         h_f32 = held.tile([P, BLOCKS, S], F32, name="h_f32")
         nc.sync.dma_start(h_f32[:], h.rearrange("(p i) s -> p i s", i=BLOCKS))
         wk_sb = held.tile([P, BLOCKS, C], BF16, name="wk_sb")
         wq_sb = held.tile([P, BLOCKS, C], BF16, name="wq_sb")
         nc.scalar.dma_start(wk_sb[:], wk.rearrange("(p i) c -> p i c", i=BLOCKS))
         nc.scalar.dma_start(wq_sb[:], wq.rearrange("(p i) c -> p i c", i=BLOCKS))
-        bk_sb = held.tile([P, BLOCKS], F32, name="bk_sb")
-        bq_sb = held.tile([P, BLOCKS], F32, name="bq_sb")
-        nc.scalar.dma_start(bk_sb[:], bk.rearrange("(b p) o -> p (b o)", p=P))
-        nc.gpsimd.dma_start(bq_sb[:], bq.rearrange("(b p) o -> p (b o)", p=P))
+        for m, vector in enumerate((bk, bq)):
+            nc.sync.dma_start(first_rows[:, m], vector.rearrange("(b g x) o -> g b (x o)", b=BLOCKS, x=SQUARE))
         offsets = held.tile([P, N // 16], U16, name="offsets")
         nc.sync.dma_start(offsets[:], offs)
 
@@ -54,13 +57,17 @@ def tile_attentionfusion_kernel(tc, h, wq, bq, wk, bk, offs, out):
         for repeat in range(WARM_UP):
             nc.tensor.matmul(warm_ps[:], zeros[:, 0:P], zeros[:], start=True, stop=True)
 
-        bq_scaled = held.tile([P, BLOCKS], F32, name="bq_scaled")
-        nc.gpsimd.tensor_scalar_mul(bq_scaled[:], bq_sb[:], scale)
-
         halves = [slice(0, HALF), slice(HALF, S)]
         h_bf = held.tile([P, BLOCKS, S], BF16, name="h_bf")
-        for pixels in halves:
-            nc.vector.tensor_copy(h_bf[:, :, pixels], h_f32[:, :, pixels])
+        nc.vector.tensor_copy(h_bf[:, :, halves[0]], h_f32[:, :, halves[0]])
+        bias_cols = held.tile([P, 2, BLOCKS, SQUARE], F32, name="bias_cols", align_bytes=64)
+        nc.vector.transpose(bias_cols[:], bias_rows[:])
+        nc.vector.tensor_copy(h_bf[:, :, halves[1]], h_f32[:, :, halves[1]])
+
+        bk_sb = bias_cols[:, 0, :, 0]
+        bq_sb = bias_cols[:, 1, :, 0]
+        bq_scaled = held.tile([P, BLOCKS], F32, name="bq_scaled")
+        nc.gpsimd.tensor_scalar_mul(bq_scaled[:], bq_sb, scale)
 
         for b in range(BLOCKS):
             channels = slice(b * P, (b + 1) * P)

@@ -42,12 +42,12 @@ def tile_attentionfusion_kernel(tc, h, wq, bq, wk, bk, offs, out):
 
         h_f32 = held.tile([P, BLOCKS, S], F32, name="h_f32")
         nc.sync.dma_start(h_f32[:], h.rearrange("(p i) s -> p i s", i=BLOCKS))
-        wk_sb = held.tile([P, BLOCKS, C], BF16, name="wk_sb")
-        wq_sb = held.tile([P, BLOCKS, C], BF16, name="wq_sb")
-        nc.scalar.dma_start(wk_sb[:], wk.rearrange("(p i) c -> p i c", i=BLOCKS))
-        nc.scalar.dma_start(wq_sb[:], wq.rearrange("(p i) c -> p i c", i=BLOCKS))
         for m, vector in enumerate((bk, bq)):
             nc.sync.dma_start(first_rows[:, m], vector.rearrange("(b g x) o -> g b (x o)", b=BLOCKS, x=SQUARE))
+        wk_sb = held.tile([P, BLOCKS, C], BF16, name="wk_sb")
+        wq_sb = held.tile([P, BLOCKS, C], BF16, name="wq_sb")
+        nc.sync.dma_start(wk_sb[:], wk.rearrange("(p i) c -> p i c", i=BLOCKS))
+        nc.sync.dma_start(wq_sb[:], wq.rearrange("(p i) c -> p i c", i=BLOCKS))
         offsets = held.tile([P, N // 16], U16, name="offsets")
         nc.sync.dma_start(offsets[:], offs)
 
@@ -76,19 +76,19 @@ def tile_attentionfusion_kernel(tc, h, wq, bq, wk, bk, offs, out):
             q = held.tile([P, S], F32, name=f"q_{b}")
             for n, pixels in enumerate(halves if b == 0 else [slice(0, S)]):
                 width = pixels.stop - pixels.start
-                key_ps = banks.tile([P, width], F32, name=f"key_ps_{b}_{n}")
-                q_ps = banks.tile([P, width], F32, name=f"q_ps_{b}_{n}")
+                key_ps = banks.tile([P, S], F32, name=f"key_ps_{n}")[:, 0:width]
+                q_ps = banks.tile([P, S], F32, name=f"q_ps_{n}")[:, 0:width]
                 for bank, weights in ((key_ps, wk_sb), (q_ps, wq_sb)):
                     for i in range(BLOCKS):
                         nc.tensor.matmul(
-                            bank[:], weights[:, i, channels], h_bf[:, i, pixels], start=(i == 0), stop=(i == BLOCKS - 1)
+                            bank, weights[:, i, channels], h_bf[:, i, pixels], start=(i == 0), stop=(i == BLOCKS - 1)
                         )
                 if b == 0:
-                    nc.vector.tensor_scalar_add(key[:, pixels], key_ps[:], bk_sb[:, b : b + 1])
-                    nc.vector.tensor_scalar(q[:, pixels], q_ps[:], bq_sb[:, b : b + 1], scale, ADD, MULT)
+                    nc.vector.tensor_scalar_add(key[:, pixels], key_ps, bk_sb[:, b : b + 1])
+                    nc.vector.tensor_scalar(q[:, pixels], q_ps, bq_sb[:, b : b + 1], scale, ADD, MULT)
                 else:
-                    nc.scalar.activation(key[:, pixels], key_ps[:], IDENTITY, bias=bk_sb[:, b : b + 1])
-                    nc.scalar.activation(q[:, pixels], q_ps[:], IDENTITY, bias=bq_scaled[:, b : b + 1], scale=scale)
+                    nc.scalar.activation(key[:, pixels], key_ps, IDENTITY, bias=bk_sb[:, b : b + 1])
+                    nc.scalar.activation(q[:, pixels], q_ps, IDENTITY, bias=bq_scaled[:, b : b + 1], scale=scale)
 
             for first in range(0, NEIGHBOURS, PAIR):
                 together = min(PAIR, NEIGHBOURS - first)

@@ -11,7 +11,7 @@ N = NEIGHBOURS * S
 BLOCKS = C // P
 LIST_COLS = S // 16
 PAIR = 2
-HALF = S // 2
+PIECES = [slice(0, 192), slice(192, 384), slice(384, S)]
 STORES = BLOCKS * ((NEIGHBOURS + PAIR - 1) // PAIR)
 
 SQUARE = 32
@@ -42,8 +42,8 @@ def tile_attentionfusion_kernel(tc, h, wq, bq, wk, bk, offs, out):
 
         h_f32 = held.tile([P, BLOCKS, S], F32, name="h_f32")
         nc.sync.dma_start(h_f32[:], h.rearrange("(p i) s -> p i s", i=BLOCKS))
-        for m, vector in enumerate((bk, bq)):
-            nc.sync.dma_start(first_rows[:, m], vector.rearrange("(b g x) o -> g b (x o)", b=BLOCKS, x=SQUARE))
+        for m, (queue, vector) in enumerate(((nc.scalar, bk), (nc.sync, bq))):
+            queue.dma_start(first_rows[:, m], vector.rearrange("(b g x) o -> g b (x o)", b=BLOCKS, x=SQUARE))
         wk_sb = held.tile([P, BLOCKS, C], BF16, name="wk_sb")
         wq_sb = held.tile([P, BLOCKS, C], BF16, name="wq_sb")
         nc.sync.dma_start(wk_sb[:], wk.rearrange("(p i) c -> p i c", i=BLOCKS))
@@ -51,18 +51,24 @@ def tile_attentionfusion_kernel(tc, h, wq, bq, wk, bk, offs, out):
         offsets = held.tile([P, N // 16], U16, name="offsets")
         nc.sync.dma_start(offsets[:], offs)
 
-        zeros = held.tile([P, S], BF16, name="zeros")
+        zeros = held.tile([P, P], BF16, name="zeros")
         nc.vector.memset(zeros[:], 0.0)
         warm_ps = banks.tile([P, S], F32, name="warm_ps")
         for repeat in range(WARM_UP):
-            nc.tensor.matmul(warm_ps[:], zeros[:, 0:P], zeros[:], start=True, stop=True)
+            nc.tensor.matmul(
+                warm_ps[:].rearrange("p (r c) -> p r c", c=P),
+                zeros[:],
+                zeros[:].unsqueeze(1).to_broadcast([P, S // P, P]),
+                start=True,
+                stop=True,
+            )
 
-        halves = [slice(0, HALF), slice(HALF, S)]
         h_bf = held.tile([P, BLOCKS, S], BF16, name="h_bf")
-        nc.vector.tensor_copy(h_bf[:, :, halves[0]], h_f32[:, :, halves[0]])
+        nc.vector.tensor_copy(h_bf[:, :, PIECES[0]], h_f32[:, :, PIECES[0]])
+        for pixels in PIECES[1:]:
+            nc.scalar.copy(h_bf[:, :, pixels], h_f32[:, :, pixels])
         bias_cols = held.tile([P, 2, BLOCKS, SQUARE], F32, name="bias_cols", align_bytes=64)
         nc.vector.transpose(bias_cols[:], bias_rows[:])
-        nc.vector.tensor_copy(h_bf[:, :, halves[1]], h_f32[:, :, halves[1]])
 
         bk_sb = bias_cols[:, 0, :, 0]
         bq_sb = bias_cols[:, 1, :, 0]
@@ -74,7 +80,7 @@ def tile_attentionfusion_kernel(tc, h, wq, bq, wk, bk, offs, out):
 
             key = held.tile([P, S], F32, name=f"key_{b}")
             q = held.tile([P, S], F32, name=f"q_{b}")
-            for n, pixels in enumerate(halves if b == 0 else [slice(0, S)]):
+            for n, pixels in enumerate(PIECES if b == 0 else [slice(0, S)]):
                 width = pixels.stop - pixels.start
                 key_ps = banks.tile([P, S], F32, name=f"key_ps_{n}")[:, 0:width]
                 q_ps = banks.tile([P, S], F32, name=f"q_ps_{n}")[:, 0:width]

import math

import concourse.mybir as mybir

P = 128
C = 256
S = 512
NEIGHBOURS = 9
HEAD = 32
N = NEIGHBOURS * S
BLOCKS = C // P
LIST_COLS = S // 16
PAIR = 2
PIECES = [slice(0, 192), slice(192, 384), slice(384, S)]
STORES = BLOCKS * ((NEIGHBOURS + PAIR - 1) // PAIR)

SQUARE = 32
WARM_UP = 4

FLOPS = 2 * 2 * C * C * S + C * N

F32 = mybir.dt.float32
BF16 = mybir.dt.bfloat16
U16 = mybir.dt.uint16
IDENTITY = mybir.ActivationFunctionType.Identity
MULT = mybir.AluOpType.mult
ADD = mybir.AluOpType.add


def tile_attentionfusion_kernel(tc, h, wq, bq, wk, bk, offs, out):
    nc = tc.nc
    scale = 1.0 / math.sqrt(HEAD)

    with (
        tc.tile_pool(name="held", bufs=1) as held,
        tc.tile_pool(name="products", bufs=STORES) as products,
        tc.psum_pool(name="banks", bufs=1) as banks,
    ):
        bias_rows = held.tile([P, 2, BLOCKS, SQUARE], F32, name="bias_rows", align_bytes=64)
        nc.vector.memset(bias_rows[:], 0.0)
        first_rows = bias_rows[:].rearrange("(g r) m b x -> g r m b x", r=SQUARE)[:, 0]

        h_f32 = held.tile([P, BLOCKS, S], F32, name="h_f32")
        nc.sync.dma_start(h_f32[:], h.rearrange("(p i) s -> p i s", i=BLOCKS))
        for m, (queue, vector) in enumerate(((nc.scalar, bk), (nc.sync, bq))):
            queue.dma_start(first_rows[:, m], vector.rearrange("(b g x) o -> g b (x o)", b=BLOCKS, x=SQUARE))
        wk_sb = held.tile([P, BLOCKS, C], BF16, name="wk_sb")
        wq_sb = held.tile([P, BLOCKS, C], BF16, name="wq_sb")
        nc.sync.dma_start(wk_sb[:], wk.rearrange("(p i) c -> p i c", i=BLOCKS))
        nc.sync.dma_start(wq_sb[:], wq.rearrange("(p i) c -> p i c", i=BLOCKS))
        offsets = held.tile([P, N // 16], U16, name="offsets")
        nc.sync.dma_start(offsets[:], offs)

        zeros = held.tile([P, P], BF16, name="zeros")
        nc.vector.memset(zeros[:], 0.0)
        warm_ps = banks.tile([P, S], F32, name="warm_ps")
        for repeat in range(WARM_UP):
            nc.tensor.matmul(
                warm_ps[:].rearrange("p (r c) -> p r c", c=P),
                zeros[:],
                zeros[:].unsqueeze(1).to_broadcast([P, S // P, P]),
                start=True,
                stop=True,
            )

        h_bf = held.tile([P, BLOCKS, S], BF16, name="h_bf")
        nc.vector.tensor_copy(h_bf[:, :, PIECES[0]], h_f32[:, :, PIECES[0]])
        for pixels in PIECES[1:]:
            nc.scalar.copy(h_bf[:, :, pixels], h_f32[:, :, pixels])
        bias_cols = held.tile([P, 2, BLOCKS, SQUARE], F32, name="bias_cols", align_bytes=64)
        nc.vector.transpose(bias_cols[:], bias_rows[:])

        bk_sb = bias_cols[:, 0, :, 0]
        bq_sb = bias_cols[:, 1, :, 0]
        bq_scaled = held.tile([P, BLOCKS], F32, name="bq_scaled")
        nc.gpsimd.tensor_scalar_mul(bq_scaled[:], bq_sb, scale)

        for b in range(BLOCKS):
            channels = slice(b * P, (b + 1) * P)

            key = held.tile([P, S], F32, name=f"key_{b}")
            q = held.tile([P, S], F32, name=f"q_{b}")
            for n, pixels in enumerate(PIECES if b == 0 else [slice(0, S)]):
                width = pixels.stop - pixels.start
                key_ps = banks.tile([P, S], F32, name=f"key_ps_{n}")[:, 0:width]
                q_ps = banks.tile([P, S], F32, name=f"q_ps_{n}")[:, 0:width]
                for bank, weights in ((key_ps, wk_sb), (q_ps, wq_sb)):
                    for i in range(BLOCKS):
                        nc.tensor.matmul(
                            bank, weights[:, i, channels], h_bf[:, i, pixels], start=(i == 0), stop=(i == BLOCKS - 1)
                        )
                if b == 0:
                    nc.vector.tensor_scalar_add(key[:, pixels], key_ps, bk_sb[:, b : b + 1])
                    nc.vector.tensor_scalar(q[:, pixels], q_ps, bq_sb[:, b : b + 1], scale, ADD, MULT)
                else:
                    nc.scalar.activation(key[:, pixels], key_ps, IDENTITY, bias=bk_sb[:, b : b + 1])
                    nc.scalar.activation(q[:, pixels], q_ps, IDENTITY, bias=bq_scaled[:, b : b + 1], scale=scale)

            for first in range(0, NEIGHBOURS, PAIR):
                together = min(PAIR, NEIGHBOURS - first)
                product = products.tile([P, together * S], F32, name="product")
                for u in range(together):
                    t = first + u
                    nc.vector.tensor_tensor(
                        product[:, u * S : (u + 1) * S],
                        key[:].indirect(offsets[:, t * LIST_COLS : (t + 1) * LIST_COLS]),
                        q[:],
                        MULT,
                    )
                nc.sync.dma_start(out[channels, first * S : (first + together) * S], product[:])
